import numpy as np
import ml_dtypes


def mxq(x, axis, fmt="e4m3"):
    dtype, down = {"e4m3": (ml_dtypes.float8_e4m3fn, 7), "e5m2": (ml_dtypes.float8_e5m2, 14)}[fmt]
    v = np.moveaxis(np.asarray(x, np.float32).astype(ml_dtypes.bfloat16).astype(np.float64), axis, -1)
    blocks = v.reshape(v.shape[:-1] + (-1, 32))
    amax = np.abs(blocks).max(-1, keepdims=True)
    byte = np.maximum(np.where(amax > 0, np.frexp(amax)[1] - 1 + 127, 0) - down, 1)
    scale = np.exp2(byte - 127.0)
    codes = (blocks / scale).astype(np.float32).astype(dtype).astype(np.float64)
    return np.moveaxis((codes * scale).reshape(v.shape), -1, axis)


WIDE = False


def mx_kscale(k):
    if not WIDE:
        return np.ones(k)
    levels = np.array([10, -10, 5, -5, 0])
    if k % 512:
        return np.exp2(np.random.permutation(np.resize(levels, k // 32))).repeat(32)
    a = np.empty((k // 512, 16))
    for p in range(k // 512):
        a[p, :8] = np.random.permutation(np.resize(levels, 8))
        for g in range(8):
            far = levels[np.abs(levels - a[p, g]) >= 10]
            a[p, g + 8] = far[np.random.randint(len(far))]
    return np.exp2(a.ravel()).repeat(32)


BF16 = ml_dtypes.bfloat16


def bf(x):
    return np.asarray(x, np.float32).astype(BF16)


def f64(x):
    return np.asarray(x).astype(np.float64)


B, S, DV, D, H, A = 4, 1024, 1024, 256, 2, 64
LN_EPS = 1e-3


def setup_inputs():
    s = mx_kscale(DV)
    return {
        "attn": bf(np.random.standard_normal((B, H, S, DV)) * 0.4 * s),
        "Wo": bf(np.random.standard_normal((H, DV, D)) * 0.6 / np.sqrt(DV * H) / s[None, :, None]),
        "bo": bf(np.random.standard_normal((H, D)) * 0.12 / np.sqrt(H)),
        "query_inputs": bf(np.random.standard_normal((B, S, D)) * 0.1),
        "gamma": bf(1.0 + 0.1 * np.random.standard_normal(D)),
        "beta": bf(0.1 * np.random.standard_normal(D)),
    }


def reference(attn, Wo, bo, query_inputs, gamma, beta):
    pre = mxq(f64(attn), 3, "e4m3") @ mxq(f64(Wo), 1, "e4m3")
    head_out = np.maximum(pre + f64(bo)[None, :, None, :], 0.0)
    x = f64(query_inputs) + head_out.sum(axis=1)
    mean = x.mean(axis=-1, keepdims=True)
    var = x.var(axis=-1, keepdims=True)
    return f64(gamma) * (x - mean) / np.sqrt(var + LN_EPS) + f64(beta)

@@ -1,0 +1,342 @@
+from contextlib import ExitStack
+
+import concourse.mybir as mybir
+from concourse.masks import make_identity
+
+F32 = mybir.dt.float32
+BF16 = mybir.dt.bfloat16
+U32 = mybir.dt.uint32
+U8 = mybir.dt.uint8
+FP8X4 = mybir.dt.float8_e4m3fn_x4
+ALU = mybir.AluOpType
+ACT = mybir.ActivationFunctionType
+
+B, H, S, DV, D = 4, 2, 1024, 1024, 256
+LN_EPS = 1e-3
+FLOPS = 2 * B * H * S * DV * D
+
+P = 128
+NSTEP = 32
+NBLK = 16
+XBUFS = 18
+AHEAD = 14
+V_EV = ()
+Q_LEAD = 3
+V_EVERY = 100
+HS_VC = 128
+
+
+def tile_multiheadattentionunit_pa_t_kernel(tc, attn, Wo, bo, query_inputs, gamma, beta, out):
+    nc = tc.nc
+    with ExitStack() as ctx:
+        const = ctx.enter_context(tc.tile_pool(name="const", bufs=1))
+        xpool = ctx.enter_context(tc.tile_pool(name="xpool", bufs=XBUFS))
+        work = ctx.enter_context(tc.tile_pool(name="work", bufs=3))
+        stat = ctx.enter_context(tc.tile_pool(name="stat", bufs=6))
+        psum = ctx.enter_context(tc.psum_pool(name="psum", bufs=1))
+        ctx.enter_context(tc.manual_schedule())
+
+        xin = {}
+        grps = {}
+        banks = {}
+        codes = {}
+        scls = {}
+        pps = {}
+        rs = {}
+        tbs = {}
+        ys = {}
+        outs = {}
+        st = {}
+        qts = {}
+
+        def load(s, parts):
+            blk, h = s // 2, s % 2
+            x = xpool.tile([P, 2, DV], BF16, name="xin", tag="xin")
+            r0 = (blk % 4) * 256
+            src = attn[blk // 4, h, r0:r0 + 256, :].rearrange("(p j) k -> p j k", j=2)
+            w = DV // parts
+            for i in range(parts):
+                nc.sync.dma_start(out=x[:, :, i * w:(i + 1) * w], in_=src[:, :, i * w:(i + 1) * w])
+            xin[s] = x
+
+        def load_q(blk):
+            qt = work.tile([P, 2, D], BF16, name="qt", tag="qt", bufs=10)
+            r0 = (blk % 4) * 256
+            nc.sync.dma_start(out=qt[:], in_=query_inputs[blk // 4, r0:r0 + 256, :].rearrange("(p j) d -> p j d", j=2))
+            qts[blk] = qt
+
+        load(0, 2)
+
+        gbrow = const.tile([P, 2 * D], BF16, name="gbrow")
+        nc.vector.memset(gbrow[:], 0.0)
+        zb = const.tile([P, P], BF16, name="zb")
+        nc.vector.memset(zb[:], 0.0)
+        nc.scalar.dma_start(out=zb[0:4, :], in_=bo.rearrange("h (c p) -> (h c) p", p=P))
+        nc.scalar.dma_start(out=gbrow[0:1, 0:D], in_=gamma.rearrange("(o d) -> o d", o=1))
+        nc.scalar.dma_start(out=gbrow[0:1, D:2 * D], in_=beta.rearrange("(o d) -> o d", o=1))
+        one_t = const.tile([P, 1], F32, name="one_t")
+        nc.vector.memset(one_t[:], 1.0)
+        eps_t = const.tile([P, 1], F32, name="eps_t")
+        nc.vector.tensor_scalar(out=eps_t[:], in0=one_t[:], scalar1=LN_EPS, scalar2=None, op0=ALU.mult)
+        scr = const.tile([P, 1], F32, name="scr")
+        nc.scalar.activation(out=scr[:], in_=eps_t[:], func=ACT.Sqrt)
+        ident_f = const.tile([P, P], F32, name="ident_f")
+        make_identity(nc, ident_f[:])
+        ident_b = const.tile([P, P], BF16, name="ident_b")
+        make_identity(nc, ident_b[:])
+        ones_b = const.tile([P, P], BF16, name="ones_b")
+        nc.gpsimd.memset(ones_b[:], 1.0)
+
+        wraw = const.tile([P, 4, 4, D], BF16, name="wraw")
+        wcodes = const.tile([P, 4, D], U32, name="wcodes", align_bytes=64)
+        wscl = const.tile([P, 4, D], U8, name="wscl", align_bytes=64)
+        wgrp = const.tile([P, 4, D, 4], BF16, name="wgrp", align_bytes=64)
+        gb = const.tile([P, 2 * D], F32, name="gb")
+        bias_f = const.tile([P, 4], F32, name="bias_f")
+        gam = gb[:, 0:D]
+        bet = gb[:, D:2 * D]
+
+        def load_w(h):
+            nc.sync.dma_start(
+                out=wraw[:, 2 * h:2 * h + 2, :, :].rearrange("p a t c -> p a (t c)"),
+                in_=Wo[h].rearrange("(g p t) c -> p g (t c)", g=2, p=P, t=4),
+            )
+
+        def regroup_w(a, eng):
+            src = wraw[:, a, :, :].rearrange("p t c -> p c t")
+            if eng == "v":
+                nc.vector.tensor_copy(out=wgrp[:, a, :, :], in_=src)
+            else:
+                nc.scalar.copy(out=wgrp[:, a, :, :], in_=src)
+
+        def quant_w(a):
+            nc.vector.quantize_mx(
+                out=wcodes[:, a, :].bitcast(FP8X4),
+                scales=wscl[:, a, :],
+                in_=wgrp[:, a, :, :].rearrange("p c t -> p (c t)"),
+            )
+
+        bps = psum.tile([P, P], BF16, name="bps", tag="tb", bufs=2)
+
+        def const_bias_t():
+            nc.tensor.transpose(bps[:], zb[:], ident_b[:])
+
+        def const_bias_c():
+            nc.vector.tensor_copy(out=bias_f[:], in_=bps[:, 0:4])
+
+        cps = psum.tile([P, 2 * D], F32, name="cps", tag="tb", bufs=2)
+
+        def const_gb_m():
+            nc.tensor.matmul(cps[:], lhsT=ones_b[:], rhs=gbrow[:], start=True, stop=True)
+
+        def const_gb_c():
+            nc.vector.tensor_copy(out=gb[:], in_=cps[:])
+
+        def tf(s):
+            grps[s] = work.tile([P, 512, 2], F32, name="grp", tag="grp", bufs=4, align_bytes=64)
+            for g in range(2):
+                bank = psum.tile([P, 2, 2, P], F32, name="tf", tag="tf", bufs=4)
+                banks[(s, g)] = bank
+                for u in range(2):
+                    for jj in range(2):
+                        nc.tensor.transpose(bank[:, u, jj, :], xin[s][:, jj, :].bitcast(F32)[:, 256 * g + u:256 * (g + 1):2], ident_f[:])
+
+        def evac(s, g, on_vector):
+            src = banks[(s, g)][:].rearrange("p u j r -> p (j r) u")
+            dst = grps[s][:, g * 256:(g + 1) * 256, :]
+            if on_vector:
+                nc.vector.tensor_copy(out=dst, in_=src)
+            else:
+                nc.scalar.copy(out=dst, in_=src)
+
+        def quant(s):
+            ac = work.tile([P, 512], U32, name="ac", tag="ac", bufs=5, align_bytes=64)
+            asc = work.tile([P, 512], U8, name="asc", tag="asc", bufs=5, align_bytes=64)
+            nc.vector.quantize_mx(
+                out=ac[:].bitcast(FP8X4),
+                scales=asc[:],
+                in_=grps[s][:].rearrange("p c u -> p (c u)").bitcast(BF16),
+            )
+            codes[s] = ac
+            scls[s] = asc
+
+        def mm(s):
+            h = s % 2
+            if s >= NSTEP - 2:
+                pps[s] = psum.tile([P, 2, 256], F32, name="pp", tag="tf", bufs=4)
+            else:
+                pps[s] = psum.tile([P, 2, 256], F32, name="pp", tag="pp", bufs=2)
+            for dh in range(2):
+                for g in range(2):
+                    nc.tensor.matmul_mx(
+                        out=pps[s][:, dh, :],
+                        lhsT=wcodes[:, 2 * h + g, dh * P:(dh + 1) * P].bitcast(FP8X4),
+                        lhsT_scale=wscl[:, 2 * h + g, dh * P:(dh + 1) * P],
+                        rhs=codes[s][:, g * 256:(g + 1) * 256].bitcast(FP8X4),
+                        rhs_scale=scls[s][:, g * 256:(g + 1) * 256],
+                        start=(g == 0),
+                        stop=(g == 1),
+                    )
+
+        def relu(blk):
+            for h in range(2):
+                rs[2 * blk + h] = work.tile([P, 2, 256], F32, name="r%d" % h, tag="r%d" % h, bufs=3)
+            for dh in (1, 0):
+                for h in range(2):
+                    s = 2 * blk + h
+                    nc.scalar.activation(out=rs[s][:, dh, :], in_=pps[s][:, dh, :], func=ACT.Relu,
+                                         bias=bias_f[:, 2 * h + dh:2 * h + dh + 1], scale=1.0)
+
+        def hsum(blk):
+            a, b = rs[2 * blk], rs[2 * blk + 1]
+            if HS_VC > 0:
+                nc.vector.tensor_tensor(out=a[:, 1, 0:HS_VC], in0=a[:, 1, 0:HS_VC], in1=b[:, 1, 0:HS_VC], op=ALU.add)
+            if HS_VC < 256:
+                nc.gpsimd.tensor_tensor(out=a[:, 1, HS_VC:256], in0=a[:, 1, HS_VC:256], in1=b[:, 1, HS_VC:256], op=ALU.add)
+            nc.gpsimd.tensor_tensor(out=a[:, 0, :], in0=a[:, 0, :], in1=b[:, 0, :], op=ALU.add)
+
+        def tback(blk, heads):
+            if heads == 1:
+                tb = psum.tile([P, 2, D], F32, name="tb", tag="tb", bufs=2)
+            else:
+                tb = psum.tile([P, 2, D], F32, name="tb", tag="tf", bufs=4)
+            tbs[blk] = tb
+            nc.tensor.matmul(tb[:].rearrange("p j d -> p (j d)"), lhsT=ident_b[:],
+                             rhs=qts[blk][:].rearrange("p j d -> p (j d)"), start=True, stop=False)
+            for jj in range(2):
+                for dh in range(2):
+                    for h in range(heads):
+                        nc.tensor.matmul(tb[:, jj, dh * P:(dh + 1) * P], lhsT=rs[2 * blk + h][:, dh, jj * P:(jj + 1) * P],
+                                         rhs=ident_f[:], is_transpose=True, start=False,
+                                         stop=(jj == 1 and dh == 1 and h == heads - 1))
+
+        def stats(blk):
+            st[blk] = dict(
+                bn=stat.tile([P, 2, 6], F32, name="bn", tag="bn"),
+                mv=stat.tile([P, 2, 2], F32, name="mv", tag="mv"),
+                sd=stat.tile([P, 2], F32, name="sd", tag="sd"),
+                rstd=stat.tile([P, 2], F32, name="rstd", tag="rstd"),
+            )
+            for jj in (1, 0):
+                nc.vector.bn_stats(out=st[blk]["bn"][:, jj, :], in_=tbs[blk][:, jj, :])
+
+        def aggr(blk):
+            for jj in (1, 0):
+                nc.vector.bn_aggr(out=st[blk]["mv"][:, jj, :], in_=st[blk]["bn"][:, jj, :])
+
+        def sqrt(blk):
+            nc.scalar.activation(out=st[blk]["sd"][:], in_=st[blk]["mv"][:, :, 1], func=ACT.Sqrt, bias=eps_t[:, 0:1], scale=1.0)
+
+        def recip(blk):
+            nc.vector.reciprocal(out=st[blk]["rstd"][:], in_=st[blk]["sd"][:])
+
+        def norm1(blk):
+            ys[blk] = work.tile([P, 2, D], F32, name="y", tag="y", bufs=3)
+            for jj in range(2):
+                nc.vector.scalar_tensor_tensor(out=ys[blk][:, jj, :], in0=tbs[blk][:, jj, :], scalar=st[blk]["mv"][:, jj, 0:1],
+                                               in1=gam, op0=ALU.subtract, op1=ALU.mult)
+
+        def norm2(blk):
+            o = work.tile([P, 2, D], F32, name="o", tag="o", bufs=8)
+            r0 = (blk % 4) * 256
+            dst = out[blk // 4, r0:r0 + 256, :].rearrange("(p j) d -> p j d", j=2)
+            for jj in range(2):
+                nc.vector.scalar_tensor_tensor(out=o[:, jj, :], in0=ys[blk][:, jj, :], scalar=st[blk]["rstd"][:, jj:jj + 1],
+                                               in1=bet, op0=ALU.mult, op1=ALU.add)
+                if blk == NBLK - 1:
+                    nc.sync.dma_start(out=dst[:, jj:jj + 1, :], in_=o[:, jj:jj + 1, :])
+            if blk < NBLK - 1:
+                nc.sync.dma_start(out=dst, in_=o[:])
+
+        def ok(b):
+            return 0 <= b < NBLK
+
+        def loads_for(s):
+            load(s, 1)
+            if s % 2 == 1 and ok((s - Q_LEAD) // 2):
+                load_q((s - Q_LEAD) // 2)
+
+        load_w(0)
+        load(1, 1)
+        load_w(1)
+        for s in range(2, AHEAD):
+            loads_for(s)
+
+        for k in range(NBLK):
+            e, o = 2 * k, 2 * k + 1
+            for s in (e + AHEAD, o + AHEAD):
+                if s < NSTEP:
+                    loads_for(s)
+                elif s % 2 == 1 and ok((s - Q_LEAD) // 2):
+                    load_q((s - Q_LEAD) // 2)
+            if ok(k - 1):
+                quant(o - 2)
+            if k == 1:
+                quant_w(2)
+                quant_w(3)
+            tf(e)
+            if k == 0:
+                const_bias_t()
+                const_gb_m()
+            tf(o)
+            if ok(k - 2):
+                hsum(k - 2)
+            if ok(k - 3):
+                stats(k - 3)
+            if ok(k - 4):
+                recip(k - 4)
+                norm1(k - 4)
+            if ok(k - 3):
+                aggr(k - 3)
+            head = k < 2
+            evac(e, 0, False)
+            evac(e, 1, head)
+            if k == 0:
+                regroup_w(0, "v")
+                regroup_w(1, "s")
+                quant(e)
+                quant_w(0)
+                quant_w(1)
+                const_bias_c()
+            evac(o, 0, False)
+            if ok(k - 3):
+                sqrt(k - 3)
+            evac(o, 1, head or k % V_EVERY == 1)
+            if k == 0:
+                regroup_w(2, "v")
+                regroup_w(3, "s")
+                const_gb_c()
+            if k > 0:
+                quant(e)
+            if ok(k - 4):
+                norm2(k - 4)
+            if k == 0:
+                mm(e)
+            if k > 1:
+                mm(e - 2)
+            if k > 0:
+                mm(o - 2)
+            if ok(k - 2):
+                tback(k - 2, 1)
+            if k == NBLK - 1:
+                mm(e)
+            if ok(k - 1):
+                relu(k - 1)
+
+        L = NBLK - 1
+        quant(2 * L + 1)
+        mm(2 * L + 1)
+        tback(L - 1, 2)
+        relu(L)
+        tback(L, 2)
+        for b in range(L - 2, L + 3):
+            if ok(b):
+                stats(b)
+            if ok(b - 1):
+                recip(b - 1)
+                norm1(b - 1)
+            if ok(b):
+                aggr(b)
+                sqrt(b)
+            if ok(b - 1):
+                norm2(b - 1)

@@ -178,14 +178,12 @@ def tile_multiheadattentionunit_pa_t_kernel(tc, attn, Wo, bo, query_inputs, gamm
                         stop=(g == 1),
                     )
 
-        def relu(blk):
-            for h in range(2):
-                rs[2 * blk + h] = work.tile([P, 2, 256], F32, name="r%d" % h, tag="r%d" % h, bufs=3)
+        def relu(s):
+            h = s % 2
+            rs[s] = work.tile([P, 2, 256], F32, name="r%d" % h, tag="r%d" % h, bufs=3)
             for dh in (1, 0):
-                for h in range(2):
-                    s = 2 * blk + h
-                    nc.scalar.activation(out=rs[s][:, dh, :], in_=pps[s][:, dh, :], func=ACT.Relu,
-                                         bias=bias_f[:, 2 * h + dh:2 * h + dh + 1], scale=1.0)
+                nc.scalar.activation(out=rs[s][:, dh, :], in_=pps[s][:, dh, :], func=ACT.Relu,
+                                     bias=bias_f[:, 2 * h + dh:2 * h + dh + 1], scale=1.0)
 
         def hsum(blk):
             a, b = rs[2 * blk], rs[2 * blk + 1]
@@ -278,6 +276,8 @@ def tile_multiheadattentionunit_pa_t_kernel(tc, attn, Wo, bo, query_inputs, gamm
             if k == 0:
                 const_bias_t()
                 const_gb_m()
+            if k > 1:
+                mm(e - 2)
             tf(o)
             if ok(k - 2):
                 hsum(k - 2)
@@ -298,6 +298,8 @@ def tile_multiheadattentionunit_pa_t_kernel(tc, attn, Wo, bo, query_inputs, gamm
                 quant_w(0)
                 quant_w(1)
                 const_bias_c()
+            if ok(k - 1):
+                relu(e - 2)
             evac(o, 0, False)
             if ok(k - 3):
                 sqrt(k - 3)
@@ -312,8 +314,6 @@ def tile_multiheadattentionunit_pa_t_kernel(tc, attn, Wo, bo, query_inputs, gamm
                 norm2(k - 4)
             if k == 0:
                 mm(e)
-            if k > 1:
-                mm(e - 2)
             if k > 0:
                 mm(o - 2)
             if ok(k - 2):
@@ -321,13 +321,14 @@ def tile_multiheadattentionunit_pa_t_kernel(tc, attn, Wo, bo, query_inputs, gamm
             if k == NBLK - 1:
                 mm(e)
             if ok(k - 1):
-                relu(k - 1)
+                relu(o - 2)
 
         L = NBLK - 1
         quant(2 * L + 1)
         mm(2 * L + 1)
         tback(L - 1, 2)
-        relu(L)
+        relu(2 * L)
+        relu(2 * L + 1)
         tback(L, 2)
         for b in range(L - 2, L + 3):
             if ok(b):

@@ -193,20 +193,16 @@ def tile_multiheadattentionunit_pa_t_kernel(tc, attn, Wo, bo, query_inputs, gamm
                 nc.gpsimd.tensor_tensor(out=a[:, 1, HS_VC:256], in0=a[:, 1, HS_VC:256], in1=b[:, 1, HS_VC:256], op=ALU.add)
             nc.gpsimd.tensor_tensor(out=a[:, 0, :], in0=a[:, 0, :], in1=b[:, 0, :], op=ALU.add)
 
-        def tback(blk, heads):
-            if heads == 1:
-                tb = psum.tile([P, 2, D], F32, name="tb", tag="tb", bufs=2)
-            else:
-                tb = psum.tile([P, 2, D], F32, name="tb", tag="tf", bufs=4)
-            tbs[blk] = tb
-            nc.tensor.matmul(tb[:].rearrange("p j d -> p (j d)"), lhsT=ident_b[:],
-                             rhs=qts[blk][:].rearrange("p j d -> p (j d)"), start=True, stop=False)
-            for jj in range(2):
-                for dh in range(2):
-                    for h in range(heads):
-                        nc.tensor.matmul(tb[:, jj, dh * P:(dh + 1) * P], lhsT=rs[2 * blk + h][:, dh, jj * P:(jj + 1) * P],
-                                         rhs=ident_f[:], is_transpose=True, start=False,
-                                         stop=(jj == 1 and dh == 1 and h == heads - 1))
+        def tback_open(blk, tag):
+            tbs[blk] = psum.tile([P, 2, D], F32, name="tb", tag=tag, bufs=2 if tag == "tb" else 4)
+
+        def tback(blk, jj, heads):
+            tb = tbs[blk]
+            for dh in range(2):
+                for h in range(heads):
+                    nc.tensor.matmul(tb[:, jj, dh * P:(dh + 1) * P], lhsT=rs[2 * blk + h][:, dh, jj * P:(jj + 1) * P],
+                                     rhs=ident_f[:], is_transpose=True, start=(dh == 0 and h == 0), stop=False)
+            nc.tensor.matmul(tb[:, jj, :], lhsT=ident_b[:], rhs=qts[blk][:, jj, :], start=False, stop=True)
 
         def stats(blk):
             st[blk] = dict(
@@ -254,90 +250,95 @@ def tile_multiheadattentionunit_pa_t_kernel(tc, attn, Wo, bo, query_inputs, gamm
             if s % 2 == 1 and ok((s - Q_LEAD) // 2):
                 load_q((s - Q_LEAD) // 2)
 
-        load_w(0)
         load(1, 1)
+        load_w(0)
+        loads_for(2)
         load_w(1)
-        for s in range(2, AHEAD):
+        for s in range(3, AHEAD):
             loads_for(s)
 
-        for k in range(NBLK):
-            e, o = 2 * k, 2 * k + 1
-            for s in (e + AHEAD, o + AHEAD):
-                if s < NSTEP:
-                    loads_for(s)
-                elif s % 2 == 1 and ok((s - Q_LEAD) // 2):
-                    load_q((s - Q_LEAD) // 2)
-            if ok(k - 1):
-                quant(o - 2)
-            if k == 1:
-                quant_w(2)
-                quant_w(3)
-            tf(e)
-            if k == 0:
+        LAG = 3
+        for s in range(NSTEP):
+            if s + AHEAD < NSTEP:
+                loads_for(s + AHEAD)
+            elif s % 2 == 1 and ok((s + AHEAD - Q_LEAD) // 2):
+                load_q((s + AHEAD - Q_LEAD) // 2)
+            half = s % 2
+            tf(s)
+            if s == 0:
                 const_bias_t()
                 const_gb_m()
-            if k > 1:
-                mm(e - 2)
-            tf(o)
-            if ok(k - 2):
-                hsum(k - 2)
-            if ok(k - 3):
-                stats(k - 3)
-            if ok(k - 4):
-                recip(k - 4)
-                norm1(k - 4)
-            if ok(k - 3):
-                aggr(k - 3)
-            head = k < 2
-            evac(e, 0, False)
-            evac(e, 1, head)
-            if k == 0:
-                regroup_w(0, "v")
+            t = s - LAG - 3
+            if t >= 0:
+                if t % 2 == 0:
+                    tback_open(t // 2, "tb")
+                tback(t // 2, t % 2, 1)
+            if s >= LAG:
+                mm(s - LAG)
+            head = s < 4
+            evac(s, 0, False)
+            if not head:
+                evac(s, 1, False)
+            if s == 1:
                 regroup_w(1, "s")
-                quant(e)
+            if s == 2:
+                regroup_w(3, "s")
+            if s >= LAG:
+                relu(s - LAG)
+            if head:
+                evac(s, 1, True)
+            if s == 1:
+                regroup_w(0, "v")
+                const_bias_c()
+            if s == 2:
                 quant_w(0)
                 quant_w(1)
-                const_bias_c()
-            if ok(k - 1):
-                relu(e - 2)
-            evac(o, 0, False)
-            if ok(k - 3):
-                sqrt(k - 3)
-            evac(o, 1, head or k % V_EVERY == 1)
-            if k == 0:
                 regroup_w(2, "v")
-                regroup_w(3, "s")
                 const_gb_c()
-            if k > 0:
-                quant(e)
-            if ok(k - 4):
-                norm2(k - 4)
-            if k == 0:
-                mm(e)
-            if k > 0:
-                mm(o - 2)
-            if ok(k - 2):
-                tback(k - 2, 1)
-            if k == NBLK - 1:
-                mm(e)
-            if ok(k - 1):
-                relu(o - 2)
+            if s == 3:
+                quant_w(2)
+                quant_w(3)
+            if s >= 1:
+                quant(s - 1)
+            b = (s - LAG - 2) // 2
+            if half == 1 and ok(b):
+                hsum(b)
+            b = (s - 8) // 2
+            if half == 0 and s >= 8:
+                if ok(b - 1):
+                    norm2(b - 1)
+                stats(b)
+            if half == 1 and s >= 9:
+                recip(b)
+                norm1(b)
+            if half == 0 and s >= 8:
+                aggr(b)
+                sqrt(b)
 
         L = NBLK - 1
         quant(2 * L + 1)
-        mm(2 * L + 1)
-        tback(L - 1, 2)
+        mm(2 * L - 1)
+        relu(2 * L - 1)
+        tback_open(L - 2, "tb")
+        tback(L - 2, 0, 1)
+        tback(L - 2, 1, 1)
+        mm(2 * L)
         relu(2 * L)
+        mm(2 * L + 1)
         relu(2 * L + 1)
-        tback(L, 2)
-        for b in range(L - 2, L + 3):
+        for b in (L - 1, L):
+            tback_open(b, "tf")
+            tback(b, 0, 2)
+            tback(b, 1, 2)
+        norm2(L - 4)
+        for b in range(L - 3, L + 2):
             if ok(b):
                 stats(b)
-            if ok(b - 1):
+            if b > L - 3:
                 recip(b - 1)
                 norm1(b - 1)
             if ok(b):
                 aggr(b)
                 sqrt(b)
-            if ok(b - 1):
+            if b > L - 3:
                 norm2(b - 1)

@@ -20,9 +20,8 @@ NSTEP = 32
 NBLK = 16
 XBUFS = 18
 AHEAD = 14
-V_EV = ()
 Q_LEAD = 3
-V_EVERY = 100
+LAG = 3
 HS_VC = 128
 
 
@@ -79,7 +78,7 @@ def tile_multiheadattentionunit_pa_t_kernel(tc, attn, Wo, bo, query_inputs, gamm
         eps_t = const.tile([P, 1], F32, name="eps_t")
         nc.vector.tensor_scalar(out=eps_t[:], in0=one_t[:], scalar1=LN_EPS, scalar2=None, op0=ALU.mult)
         scr = const.tile([P, 1], F32, name="scr")
-        nc.scalar.activation(out=scr[:], in_=eps_t[:], func=ACT.Sqrt)
+        nc.scalar.activation(out=scr[:], in_=eps_t[:], func=ACT.Abs_reciprocal_sqrt)
         ident_f = const.tile([P, P], F32, name="ident_f")
         make_identity(nc, ident_f[:])
         ident_b = const.tile([P, P], BF16, name="ident_b")
@@ -150,8 +149,8 @@ def tile_multiheadattentionunit_pa_t_kernel(tc, attn, Wo, bo, query_inputs, gamm
                 nc.scalar.copy(out=dst, in_=src)
 
         def quant(s):
-            ac = work.tile([P, 512], U32, name="ac", tag="ac", bufs=5, align_bytes=64)
-            asc = work.tile([P, 512], U8, name="asc", tag="asc", bufs=5, align_bytes=64)
+            ac = work.tile([P, 512], U32, name="ac", tag="ac", bufs=6, align_bytes=64)
+            asc = work.tile([P, 512], U8, name="asc", tag="asc", bufs=6, align_bytes=64)
             nc.vector.quantize_mx(
                 out=ac[:].bitcast(FP8X4),
                 scales=asc[:],
@@ -180,7 +179,7 @@ def tile_multiheadattentionunit_pa_t_kernel(tc, attn, Wo, bo, query_inputs, gamm
 
         def relu(s):
             h = s % 2
-            rs[s] = work.tile([P, 2, 256], F32, name="r%d" % h, tag="r%d" % h, bufs=3)
+            rs[s] = work.tile([P, 2, 256], F32, name="r%d" % h, tag="r%d" % h, bufs=4)
             for dh in (1, 0):
                 nc.scalar.activation(out=rs[s][:, dh, :], in_=pps[s][:, dh, :], func=ACT.Relu,
                                      bias=bias_f[:, 2 * h + dh:2 * h + dh + 1], scale=1.0)
@@ -196,19 +195,20 @@ def tile_multiheadattentionunit_pa_t_kernel(tc, attn, Wo, bo, query_inputs, gamm
         def tback_open(blk, tag):
             tbs[blk] = psum.tile([P, 2, D], F32, name="tb", tag=tag, bufs=2 if tag == "tb" else 4)
 
-        def tback(blk, jj, heads):
-            tb = tbs[blk]
-            for dh in range(2):
-                for h in range(heads):
-                    nc.tensor.matmul(tb[:, jj, dh * P:(dh + 1) * P], lhsT=rs[2 * blk + h][:, dh, jj * P:(jj + 1) * P],
-                                     rhs=ident_f[:], is_transpose=True, start=(dh == 0 and h == 0), stop=False)
-            nc.tensor.matmul(tb[:, jj, :], lhsT=ident_b[:], rhs=qts[blk][:, jj, :], start=False, stop=True)
+        def residual(blk, jj):
+            nc.tensor.matmul(tbs[blk][:, jj, :], lhsT=ident_b[:], rhs=qts[blk][:, jj, :], start=(jj == 0), stop=(jj == 1))
+
+        def tback(blk, heads):
+            for jj in range(2):
+                for dh in range(2):
+                    for h in range(heads):
+                        nc.tensor.matmul(tbs[blk][:, jj, dh * P:(dh + 1) * P], lhsT=rs[2 * blk + h][:, dh, jj * P:(jj + 1) * P],
+                                         rhs=ident_f[:], is_transpose=True, start=False, stop=False)
 
         def stats(blk):
             st[blk] = dict(
                 bn=stat.tile([P, 2, 6], F32, name="bn", tag="bn"),
                 mv=stat.tile([P, 2, 2], F32, name="mv", tag="mv"),
-                sd=stat.tile([P, 2], F32, name="sd", tag="sd"),
                 rstd=stat.tile([P, 2], F32, name="rstd", tag="rstd"),
             )
             for jj in (1, 0):
@@ -218,11 +218,8 @@ def tile_multiheadattentionunit_pa_t_kernel(tc, attn, Wo, bo, query_inputs, gamm
             for jj in (1, 0):
                 nc.vector.bn_aggr(out=st[blk]["mv"][:, jj, :], in_=st[blk]["bn"][:, jj, :])
 
-        def sqrt(blk):
-            nc.scalar.activation(out=st[blk]["sd"][:], in_=st[blk]["mv"][:, :, 1], func=ACT.Sqrt, bias=eps_t[:, 0:1], scale=1.0)
-
-        def recip(blk):
-            nc.vector.reciprocal(out=st[blk]["rstd"][:], in_=st[blk]["sd"][:])
+        def rsqrt(blk):
+            nc.scalar.activation(out=st[blk]["rstd"][:], in_=st[blk]["mv"][:, :, 1], func=ACT.Abs_reciprocal_sqrt, bias=eps_t[:, 0:1], scale=1.0)
 
         def norm1(blk):
             ys[blk] = work.tile([P, 2, D], F32, name="y", tag="y", bufs=3)
@@ -251,94 +248,111 @@ def tile_multiheadattentionunit_pa_t_kernel(tc, attn, Wo, bo, query_inputs, gamm
                 load_q((s - Q_LEAD) // 2)
 
         load(1, 1)
+        load(2, 1)
         load_w(0)
-        loads_for(2)
+        loads_for(3)
+        load(4, 1)
         load_w(1)
-        for s in range(3, AHEAD):
+        for s in range(5, AHEAD):
             loads_for(s)
 
-        LAG = 3
+        passes = {s + LAG: s for s in range(3, NSTEP)}
+        passes[3], passes[4], passes[5] = 0, 2, 1
+        sums = {2 * b + 5: b for b in range(1, NBLK - 2)}
+
+        L = NBLK - 1
         for s in range(NSTEP):
             if s + AHEAD < NSTEP:
                 loads_for(s + AHEAD)
             elif s % 2 == 1 and ok((s + AHEAD - Q_LEAD) // 2):
                 load_q((s + AHEAD - Q_LEAD) // 2)
-            half = s % 2
+            even = s % 2 == 0
+            head = s < 4
+
             tf(s)
-            if s == 0:
+            if s == 2:
                 const_bias_t()
                 const_gb_m()
-            t = s - LAG - 3
-            if t >= 0:
-                if t % 2 == 0:
-                    tback_open(t // 2, "tb")
-                tback(t // 2, t % 2, 1)
-            if s >= LAG:
-                mm(s - LAG)
-            head = s < 4
+            b = (s - 5) // 2
+            if even and b > 0:
+                tback(b, 1)
+            if s in passes:
+                mm(passes[s])
+            if ok(b):
+                if even and b > 0:
+                    residual(b, 1)
+                elif not even:
+                    tback_open(b, "tb")
+                    residual(b, 0)
+
             evac(s, 0, False)
             if not head:
                 evac(s, 1, False)
-            if s == 1:
-                regroup_w(1, "s")
             if s == 2:
-                regroup_w(3, "s")
-            if s >= LAG:
-                relu(s - LAG)
+                regroup_w(1, "s")
+            if s in passes:
+                relu(passes[s])
+
             if head:
                 evac(s, 1, True)
-            if s == 1:
-                regroup_w(0, "v")
-                const_bias_c()
-            if s == 2:
-                quant_w(0)
-                quant_w(1)
-                regroup_w(2, "v")
-                const_gb_c()
-            if s == 3:
-                quant_w(2)
-                quant_w(3)
-            if s >= 1:
+            if even:
+                if ok((s - 10) // 2):
+                    norm2((s - 10) // 2)
+                if s >= 1:
+                    quant(s - 1)
+                if s == 2:
+                    regroup_w(0, "v")
+                    quant_w(0)
+                    quant_w(1)
+                    const_bias_c()
+                if s == 4:
+                    regroup_w(3, "v")
+                    quant_w(2)
+                    quant_w(3)
+                if s == 6:
+                    hsum(0)
+                    tback(0, 1)
+                    residual(0, 1)
+            else:
                 quant(s - 1)
-            b = (s - LAG - 2) // 2
-            if half == 1 and ok(b):
-                hsum(b)
-            b = (s - 8) // 2
-            if half == 0 and s >= 8:
-                if ok(b - 1):
-                    norm2(b - 1)
-                stats(b)
-            if half == 1 and s >= 9:
-                recip(b)
-                norm1(b)
-            if half == 0 and s >= 8:
-                aggr(b)
-                sqrt(b)
+                if s == 3:
+                    regroup_w(2, "v")
+                    const_gb_c()
+                if ok((s - 9) // 2):
+                    norm1((s - 9) // 2)
+                if ok((s - 7) // 2):
+                    stats((s - 7) // 2)
+                if s in sums:
+                    hsum(sums[s])
+                if ok((s - 7) // 2):
+                    aggr((s - 7) // 2)
+                    rsqrt((s - 7) // 2)
 
-        L = NBLK - 1
         quant(2 * L + 1)
+        norm2(L - 4)
+        norm1(L - 3)
         mm(2 * L - 1)
         relu(2 * L - 1)
-        tback_open(L - 2, "tb")
-        tback(L - 2, 0, 1)
-        tback(L - 2, 1, 1)
+        tback(L - 2, 1)
+        residual(L - 2, 1)
+        stats(L - 2)
+        norm2(L - 3)
+        aggr(L - 2)
         mm(2 * L)
         relu(2 * L)
         mm(2 * L + 1)
         relu(2 * L + 1)
+        rsqrt(L - 2)
         for b in (L - 1, L):
             tback_open(b, "tf")
-            tback(b, 0, 2)
-            tback(b, 1, 2)
-        norm2(L - 4)
-        for b in range(L - 3, L + 2):
-            if ok(b):
-                stats(b)
-            if b > L - 3:
-                recip(b - 1)
-                norm1(b - 1)
-            if ok(b):
-                aggr(b)
-                sqrt(b)
-            if b > L - 3:
-                norm2(b - 1)
+            residual(b, 0)
+            tback(b, 2)
+            residual(b, 1)
+        norm1(L - 2)
+        for b in (L - 1, L):
+            stats(b)
+            norm2(b - 1)
+            aggr(b)
+            rsqrt(b)
+            norm1(b)
+        norm2(L)

@@ -22,7 +22,7 @@ XBUFS = 18
 AHEAD = 14
 Q_LEAD = 3
 LAG = 3
-HS_VC = 128
+HS_VC = 256
 
 
 def tile_multiheadattentionunit_pa_t_kernel(tc, attn, Wo, bo, query_inputs, gamma, beta, out):
@@ -96,10 +96,18 @@ def tile_multiheadattentionunit_pa_t_kernel(tc, attn, Wo, bo, query_inputs, gamm
         bet = gb[:, D:2 * D]
 
         def load_w(h):
-            nc.sync.dma_start(
-                out=wraw[:, 2 * h:2 * h + 2, :, :].rearrange("p a t c -> p a (t c)"),
-                in_=Wo[h].rearrange("(g p t) c -> p g (t c)", g=2, p=P, t=4),
-            )
+            for g in range(2):
+                if h == 0 or g == 0:
+                    nc.sync.dma_start(
+                        out=wraw[:, 2 * h + g, :, :].rearrange("p t c -> p (t c)"),
+                        in_=Wo[h, 512 * g:512 * (g + 1), :].rearrange("(p t) c -> p (t c)", t=4),
+                    )
+                else:
+                    for i in range(2):
+                        nc.sync.dma_start(
+                            out=wraw[i:P:2, 2 * h + g, :, :].rearrange("p (u e) c -> p u (e c)", u=2),
+                            in_=Wo[h, 512 * g:512 * (g + 1), :].rearrange("(m u i e) c -> i m u (e c)", u=2, i=2, e=2)[i],
+                        )
 
         def regroup_w(a, eng):
             src = wraw[:, a, :, :].rearrange("p t c -> p c t")
@@ -131,6 +139,15 @@ def tile_multiheadattentionunit_pa_t_kernel(tc, attn, Wo, bo, query_inputs, gamm
         def const_gb_c():
             nc.vector.tensor_copy(out=gb[:], in_=cps[:])
 
+        xps = {}
+
+        def sort(s):
+            xps[s] = work.tile([P, 2, 2, P], F32, name="xp", tag="xp", bufs=3, align_bytes=64)
+            src = xin[s][:, :, 512:1024].bitcast(F32).rearrange("p j (m u i) -> p j u m i", u=2, i=2)
+            dst = xps[s][:].rearrange("p j u (m i) -> p j u m i", i=2)
+            nc.vector.tensor_copy(out=dst[:, 0], in_=src[:, 0])
+            nc.scalar.copy(out=dst[:, 1], in_=src[:, 1])
+
         def tf(s):
             grps[s] = work.tile([P, 512, 2], F32, name="grp", tag="grp", bufs=4, align_bytes=64)
             for g in range(2):
@@ -138,7 +155,11 @@ def tile_multiheadattentionunit_pa_t_kernel(tc, attn, Wo, bo, query_inputs, gamm
                 banks[(s, g)] = bank
                 for u in range(2):
                     for jj in range(2):
-                        nc.tensor.transpose(bank[:, u, jj, :], xin[s][:, jj, :].bitcast(F32)[:, 256 * g + u:256 * (g + 1):2], ident_f[:])
+                        if s % 2 == 1 and g == 1:
+                            words = xps[s][:, jj, u, :]
+                        else:
+                            words = xin[s][:, jj, :].bitcast(F32)[:, 256 * g + u:256 * (g + 1):2]
+                        nc.tensor.transpose(bank[:, u, jj, :], words, ident_f[:])
 
         def evac(s, g, on_vector):
             src = banks[(s, g)][:].rearrange("p u j r -> p (j r) u")
@@ -261,6 +282,7 @@ def tile_multiheadattentionunit_pa_t_kernel(tc, attn, Wo, bo, query_inputs, gamm
         sums = {2 * b + 5: b for b in range(1, NBLK - 2)}
 
         L = NBLK - 1
+        sort(1)
         for s in range(NSTEP):
             if s + AHEAD < NSTEP:
                 loads_for(s + AHEAD)
@@ -274,14 +296,14 @@ def tile_multiheadattentionunit_pa_t_kernel(tc, attn, Wo, bo, query_inputs, gamm
                 const_bias_t()
                 const_gb_m()
             b = (s - 5) // 2
-            if even and b > 0:
-                tback(b, 1)
+            if even and ok(b):
+                tback(b, 1 if b > 0 else 2)
             if s in passes:
                 mm(passes[s])
             if ok(b):
-                if even and b > 0:
+                if even:
                     residual(b, 1)
-                elif not even:
+                else:
                     tback_open(b, "tb")
                     residual(b, 0)
 
@@ -296,11 +318,13 @@ def tile_multiheadattentionunit_pa_t_kernel(tc, attn, Wo, bo, query_inputs, gamm
             if head:
                 evac(s, 1, True)
             if even:
-                if ok((s - 10) // 2):
-                    norm2((s - 10) // 2)
                 if s >= 1:
                     quant(s - 1)
+                if ok((s - 8) // 2):
+                    norm1((s - 8) // 2)
+                    norm2((s - 8) // 2)
                 if s == 2:
+                    sort(3)
                     regroup_w(0, "v")
                     quant_w(0)
                     quant_w(1)
@@ -309,19 +333,15 @@ def tile_multiheadattentionunit_pa_t_kernel(tc, attn, Wo, bo, query_inputs, gamm
                     regroup_w(3, "v")
                     quant_w(2)
                     quant_w(3)
-                if s == 6:
-                    hsum(0)
-                    tback(0, 1)
-                    residual(0, 1)
             else:
                 quant(s - 1)
                 if s == 3:
                     regroup_w(2, "v")
                     const_gb_c()
-                if ok((s - 9) // 2):
-                    norm1((s - 9) // 2)
                 if ok((s - 7) // 2):
                     stats((s - 7) // 2)
+                if 5 <= s + 2 < NSTEP:
+                    sort(s + 2)
                 if s in sums:
                     hsum(sums[s])
                 if ok((s - 7) // 2):
@@ -329,19 +349,15 @@ def tile_multiheadattentionunit_pa_t_kernel(tc, attn, Wo, bo, query_inputs, gamm
                     rsqrt((s - 7) // 2)
 
         quant(2 * L + 1)
-        norm2(L - 4)
         norm1(L - 3)
-        mm(2 * L - 1)
-        relu(2 * L - 1)
         tback(L - 2, 1)
         residual(L - 2, 1)
-        stats(L - 2)
         norm2(L - 3)
+        stats(L - 2)
+        for s in range(NSTEP - LAG, NSTEP):
+            mm(s)
+            relu(s)
         aggr(L - 2)
-        mm(2 * L)
-        relu(2 * L)
-        mm(2 * L + 1)
-        relu(2 * L + 1)
         rsqrt(L - 2)
         for b in (L - 1, L):
             tback_open(b, "tf")

@@ -96,18 +96,10 @@ def tile_multiheadattentionunit_pa_t_kernel(tc, attn, Wo, bo, query_inputs, gamm
         bet = gb[:, D:2 * D]
 
         def load_w(h):
-            for g in range(2):
-                if h == 0 or g == 0:
-                    nc.sync.dma_start(
-                        out=wraw[:, 2 * h + g, :, :].rearrange("p t c -> p (t c)"),
-                        in_=Wo[h, 512 * g:512 * (g + 1), :].rearrange("(p t) c -> p (t c)", t=4),
-                    )
-                else:
-                    for i in range(2):
-                        nc.sync.dma_start(
-                            out=wraw[i:P:2, 2 * h + g, :, :].rearrange("p (u e) c -> p u (e c)", u=2),
-                            in_=Wo[h, 512 * g:512 * (g + 1), :].rearrange("(m u i e) c -> i m u (e c)", u=2, i=2, e=2)[i],
-                        )
+            nc.sync.dma_start(
+                out=wraw[:, 2 * h:2 * h + 2, :, :].rearrange("p a t c -> p a (t c)"),
+                in_=Wo[h].rearrange("(g p t) c -> p g (t c)", g=2, p=P, t=4),
+            )
 
         def regroup_w(a, eng):
             src = wraw[:, a, :, :].rearrange("p t c -> p c t")
@@ -139,15 +131,6 @@ def tile_multiheadattentionunit_pa_t_kernel(tc, attn, Wo, bo, query_inputs, gamm
         def const_gb_c():
             nc.vector.tensor_copy(out=gb[:], in_=cps[:])
 
-        xps = {}
-
-        def sort(s):
-            xps[s] = work.tile([P, 2, 2, P], F32, name="xp", tag="xp", bufs=3, align_bytes=64)
-            src = xin[s][:, :, 512:1024].bitcast(F32).rearrange("p j (m u i) -> p j u m i", u=2, i=2)
-            dst = xps[s][:].rearrange("p j u (m i) -> p j u m i", i=2)
-            nc.vector.tensor_copy(out=dst[:, 0], in_=src[:, 0])
-            nc.scalar.copy(out=dst[:, 1], in_=src[:, 1])
-
         def tf(s):
             grps[s] = work.tile([P, 512, 2], F32, name="grp", tag="grp", bufs=4, align_bytes=64)
             for g in range(2):
@@ -155,11 +138,7 @@ def tile_multiheadattentionunit_pa_t_kernel(tc, attn, Wo, bo, query_inputs, gamm
                 banks[(s, g)] = bank
                 for u in range(2):
                     for jj in range(2):
-                        if s % 2 == 1 and g == 1:
-                            words = xps[s][:, jj, u, :]
-                        else:
-                            words = xin[s][:, jj, :].bitcast(F32)[:, 256 * g + u:256 * (g + 1):2]
-                        nc.tensor.transpose(bank[:, u, jj, :], words, ident_f[:])
+                        nc.tensor.transpose(bank[:, u, jj, :], xin[s][:, jj, :].bitcast(F32)[:, 256 * g + u:256 * (g + 1):2], ident_f[:])
 
         def evac(s, g, on_vector):
             src = banks[(s, g)][:].rearrange("p u j r -> p (j r) u")
@@ -282,7 +261,6 @@ def tile_multiheadattentionunit_pa_t_kernel(tc, attn, Wo, bo, query_inputs, gamm
         sums = {2 * b + 5: b for b in range(1, NBLK - 2)}
 
         L = NBLK - 1
-        sort(1)
         for s in range(NSTEP):
             if s + AHEAD < NSTEP:
                 loads_for(s + AHEAD)
@@ -324,7 +302,6 @@ def tile_multiheadattentionunit_pa_t_kernel(tc, attn, Wo, bo, query_inputs, gamm
                     norm1((s - 8) // 2)
                     norm2((s - 8) // 2)
                 if s == 2:
-                    sort(3)
                     regroup_w(0, "v")
                     quant_w(0)
                     quant_w(1)
@@ -340,8 +317,6 @@ def tile_multiheadattentionunit_pa_t_kernel(tc, attn, Wo, bo, query_inputs, gamm
                     const_gb_c()
                 if ok((s - 7) // 2):
                     stats((s - 7) // 2)
-                if 5 <= s + 2 < NSTEP:
-                    sort(s + 2)
                 if s in sums:
                     hsum(sums[s])
                 if ok((s - 7) // 2):

from contextlib import ExitStack

import concourse.mybir as mybir
from concourse.masks import make_identity

F32 = mybir.dt.float32
BF16 = mybir.dt.bfloat16
U32 = mybir.dt.uint32
U8 = mybir.dt.uint8
FP8X4 = mybir.dt.float8_e4m3fn_x4
ALU = mybir.AluOpType
ACT = mybir.ActivationFunctionType

B, H, S, DV, D = 4, 2, 1024, 1024, 256
LN_EPS = 1e-3
FLOPS = 2 * B * H * S * DV * D

P = 128
NSTEP = 32
NBLK = 16
XBUFS = 18
AHEAD = 14
Q_LEAD = 3
LAG = 3
HS_VC = 256


def tile_multiheadattentionunit_pa_t_kernel(tc, attn, Wo, bo, query_inputs, gamma, beta, out):
    nc = tc.nc
    with ExitStack() as ctx:
        const = ctx.enter_context(tc.tile_pool(name="const", bufs=1))
        xpool = ctx.enter_context(tc.tile_pool(name="xpool", bufs=XBUFS))
        work = ctx.enter_context(tc.tile_pool(name="work", bufs=3))
        stat = ctx.enter_context(tc.tile_pool(name="stat", bufs=6))
        psum = ctx.enter_context(tc.psum_pool(name="psum", bufs=1))
        ctx.enter_context(tc.manual_schedule())

        xin = {}
        grps = {}
        banks = {}
        codes = {}
        scls = {}
        pps = {}
        rs = {}
        tbs = {}
        ys = {}
        outs = {}
        st = {}
        qts = {}

        def load(s, parts):
            blk, h = s // 2, s % 2
            x = xpool.tile([P, 2, DV], BF16, name="xin", tag="xin")
            r0 = (blk % 4) * 256
            src = attn[blk // 4, h, r0:r0 + 256, :].rearrange("(p j) k -> p j k", j=2)
            w = DV // parts
            for i in range(parts):
                nc.sync.dma_start(out=x[:, :, i * w:(i + 1) * w], in_=src[:, :, i * w:(i + 1) * w])
            xin[s] = x

        def load_q(blk):
            qt = work.tile([P, 2, D], BF16, name="qt", tag="qt", bufs=10)
            r0 = (blk % 4) * 256
            nc.sync.dma_start(out=qt[:], in_=query_inputs[blk // 4, r0:r0 + 256, :].rearrange("(p j) d -> p j d", j=2))
            qts[blk] = qt

        load(0, 2)

        gbrow = const.tile([P, 2 * D], BF16, name="gbrow")
        nc.vector.memset(gbrow[:], 0.0)
        zb = const.tile([P, P], BF16, name="zb")
        nc.vector.memset(zb[:], 0.0)
        nc.scalar.dma_start(out=zb[0:4, :], in_=bo.rearrange("h (c p) -> (h c) p", p=P))
        nc.scalar.dma_start(out=gbrow[0:1, 0:D], in_=gamma.rearrange("(o d) -> o d", o=1))
        nc.scalar.dma_start(out=gbrow[0:1, D:2 * D], in_=beta.rearrange("(o d) -> o d", o=1))
        one_t = const.tile([P, 1], F32, name="one_t")
        nc.vector.memset(one_t[:], 1.0)
        eps_t = const.tile([P, 1], F32, name="eps_t")
        nc.vector.tensor_scalar(out=eps_t[:], in0=one_t[:], scalar1=LN_EPS, scalar2=None, op0=ALU.mult)
        scr = const.tile([P, 1], F32, name="scr")
        nc.scalar.activation(out=scr[:], in_=eps_t[:], func=ACT.Abs_reciprocal_sqrt)
        ident_f = const.tile([P, P], F32, name="ident_f")
        make_identity(nc, ident_f[:])
        ident_b = const.tile([P, P], BF16, name="ident_b")
        make_identity(nc, ident_b[:])
        ones_b = const.tile([P, P], BF16, name="ones_b")
        nc.gpsimd.memset(ones_b[:], 1.0)

        wraw = const.tile([P, 4, 4, D], BF16, name="wraw")
        wcodes = const.tile([P, 4, D], U32, name="wcodes", align_bytes=64)
        wscl = const.tile([P, 4, D], U8, name="wscl", align_bytes=64)
        wgrp = const.tile([P, 4, D, 4], BF16, name="wgrp", align_bytes=64)
        gb = const.tile([P, 2 * D], F32, name="gb")
        bias_f = const.tile([P, 4], F32, name="bias_f")
        gam = gb[:, 0:D]
        bet = gb[:, D:2 * D]

        def load_w(h):
            nc.sync.dma_start(
                out=wraw[:, 2 * h:2 * h + 2, :, :].rearrange("p a t c -> p a (t c)"),
                in_=Wo[h].rearrange("(g p t) c -> p g (t c)", g=2, p=P, t=4),
            )

        def regroup_w(a, eng):
            src = wraw[:, a, :, :].rearrange("p t c -> p c t")
            if eng == "v":
                nc.vector.tensor_copy(out=wgrp[:, a, :, :], in_=src)
            else:
                nc.scalar.copy(out=wgrp[:, a, :, :], in_=src)

        def quant_w(a):
            nc.vector.quantize_mx(
                out=wcodes[:, a, :].bitcast(FP8X4),
                scales=wscl[:, a, :],
                in_=wgrp[:, a, :, :].rearrange("p c t -> p (c t)"),
            )

        bps = psum.tile([P, P], BF16, name="bps", tag="tb", bufs=2)

        def const_bias_t():
            nc.tensor.transpose(bps[:], zb[:], ident_b[:])

        def const_bias_c():
            nc.vector.tensor_copy(out=bias_f[:], in_=bps[:, 0:4])

        cps = psum.tile([P, 2 * D], F32, name="cps", tag="tb", bufs=2)

        def const_gb_m():
            nc.tensor.matmul(cps[:], lhsT=ones_b[:], rhs=gbrow[:], start=True, stop=True)

        def const_gb_c():
            nc.vector.tensor_copy(out=gb[:], in_=cps[:])

        def tf(s):
            grps[s] = work.tile([P, 512, 2], F32, name="grp", tag="grp", bufs=4, align_bytes=64)
            for g in range(2):
                bank = psum.tile([P, 2, 2, P], F32, name="tf", tag="tf", bufs=4)
                banks[(s, g)] = bank
                for u in range(2):
                    for jj in range(2):
                        nc.tensor.transpose(bank[:, u, jj, :], xin[s][:, jj, :].bitcast(F32)[:, 256 * g + u:256 * (g + 1):2], ident_f[:])

        def evac(s, g, on_vector):
            src = banks[(s, g)][:].rearrange("p u j r -> p (j r) u")
            dst = grps[s][:, g * 256:(g + 1) * 256, :]
            if on_vector:
                nc.vector.tensor_copy(out=dst, in_=src)
            else:
                nc.scalar.copy(out=dst, in_=src)

        def quant(s):
            ac = work.tile([P, 512], U32, name="ac", tag="ac", bufs=6, align_bytes=64)
            asc = work.tile([P, 512], U8, name="asc", tag="asc", bufs=6, align_bytes=64)
            nc.vector.quantize_mx(
                out=ac[:].bitcast(FP8X4),
                scales=asc[:],
                in_=grps[s][:].rearrange("p c u -> p (c u)").bitcast(BF16),
            )
            codes[s] = ac
            scls[s] = asc

        def mm(s):
            h = s % 2
            if s >= NSTEP - 2:
                pps[s] = psum.tile([P, 2, 256], F32, name="pp", tag="tf", bufs=4)
            else:
                pps[s] = psum.tile([P, 2, 256], F32, name="pp", tag="pp", bufs=2)
            for dh in range(2):
                for g in range(2):
                    nc.tensor.matmul_mx(
                        out=pps[s][:, dh, :],
                        lhsT=wcodes[:, 2 * h + g, dh * P:(dh + 1) * P].bitcast(FP8X4),
                        lhsT_scale=wscl[:, 2 * h + g, dh * P:(dh + 1) * P],
                        rhs=codes[s][:, g * 256:(g + 1) * 256].bitcast(FP8X4),
                        rhs_scale=scls[s][:, g * 256:(g + 1) * 256],
                        start=(g == 0),
                        stop=(g == 1),
                    )

        def relu(s):
            h = s % 2
            rs[s] = work.tile([P, 2, 256], F32, name="r%d" % h, tag="r%d" % h, bufs=4)
            for dh in (1, 0):
                nc.scalar.activation(out=rs[s][:, dh, :], in_=pps[s][:, dh, :], func=ACT.Relu,
                                     bias=bias_f[:, 2 * h + dh:2 * h + dh + 1], scale=1.0)

        def hsum(blk):
            a, b = rs[2 * blk], rs[2 * blk + 1]
            if HS_VC > 0:
                nc.vector.tensor_tensor(out=a[:, 1, 0:HS_VC], in0=a[:, 1, 0:HS_VC], in1=b[:, 1, 0:HS_VC], op=ALU.add)
            if HS_VC < 256:
                nc.gpsimd.tensor_tensor(out=a[:, 1, HS_VC:256], in0=a[:, 1, HS_VC:256], in1=b[:, 1, HS_VC:256], op=ALU.add)
            nc.gpsimd.tensor_tensor(out=a[:, 0, :], in0=a[:, 0, :], in1=b[:, 0, :], op=ALU.add)

        def tback_open(blk, tag):
            tbs[blk] = psum.tile([P, 2, D], F32, name="tb", tag=tag, bufs=2 if tag == "tb" else 4)

        def residual(blk, jj):
            nc.tensor.matmul(tbs[blk][:, jj, :], lhsT=ident_b[:], rhs=qts[blk][:, jj, :], start=(jj == 0), stop=(jj == 1))

        def tback(blk, heads):
            for jj in range(2):
                for dh in range(2):
                    for h in range(heads):
                        nc.tensor.matmul(tbs[blk][:, jj, dh * P:(dh + 1) * P], lhsT=rs[2 * blk + h][:, dh, jj * P:(jj + 1) * P],
                                         rhs=ident_f[:], is_transpose=True, start=False, stop=False)

        def stats(blk):
            st[blk] = dict(
                bn=stat.tile([P, 2, 6], F32, name="bn", tag="bn"),
                mv=stat.tile([P, 2, 2], F32, name="mv", tag="mv"),
                rstd=stat.tile([P, 2], F32, name="rstd", tag="rstd"),
            )
            for jj in (1, 0):
                nc.vector.bn_stats(out=st[blk]["bn"][:, jj, :], in_=tbs[blk][:, jj, :])

        def aggr(blk):
            for jj in (1, 0):
                nc.vector.bn_aggr(out=st[blk]["mv"][:, jj, :], in_=st[blk]["bn"][:, jj, :])

        def rsqrt(blk):
            nc.scalar.activation(out=st[blk]["rstd"][:], in_=st[blk]["mv"][:, :, 1], func=ACT.Abs_reciprocal_sqrt, bias=eps_t[:, 0:1], scale=1.0)

        def norm1(blk):
            ys[blk] = work.tile([P, 2, D], F32, name="y", tag="y", bufs=3)
            for jj in range(2):
                nc.vector.scalar_tensor_tensor(out=ys[blk][:, jj, :], in0=tbs[blk][:, jj, :], scalar=st[blk]["mv"][:, jj, 0:1],
                                               in1=gam, op0=ALU.subtract, op1=ALU.mult)

        def norm2(blk):
            o = work.tile([P, 2, D], F32, name="o", tag="o", bufs=8)
            r0 = (blk % 4) * 256
            dst = out[blk // 4, r0:r0 + 256, :].rearrange("(p j) d -> p j d", j=2)
            for jj in range(2):
                nc.vector.scalar_tensor_tensor(out=o[:, jj, :], in0=ys[blk][:, jj, :], scalar=st[blk]["rstd"][:, jj:jj + 1],
                                               in1=bet, op0=ALU.mult, op1=ALU.add)
                if blk == NBLK - 1:
                    nc.sync.dma_start(out=dst[:, jj:jj + 1, :], in_=o[:, jj:jj + 1, :])
            if blk < NBLK - 1:
                nc.sync.dma_start(out=dst, in_=o[:])

        def ok(b):
            return 0 <= b < NBLK

        def loads_for(s):
            load(s, 1)
            if s % 2 == 1 and ok((s - Q_LEAD) // 2):
                load_q((s - Q_LEAD) // 2)

        load(1, 1)
        load(2, 1)
        load_w(0)
        loads_for(3)
        load(4, 1)
        load_w(1)
        for s in range(5, AHEAD):
            loads_for(s)

        passes = {s + LAG: s for s in range(3, NSTEP)}
        passes[3], passes[4], passes[5] = 0, 2, 1
        sums = {2 * b + 5: b for b in range(1, NBLK - 2)}

        L = NBLK - 1
        for s in range(NSTEP):
            if s + AHEAD < NSTEP:
                loads_for(s + AHEAD)
            elif s % 2 == 1 and ok((s + AHEAD - Q_LEAD) // 2):
                load_q((s + AHEAD - Q_LEAD) // 2)
            even = s % 2 == 0
            head = s < 4

            tf(s)
            if s == 2:
                const_bias_t()
                const_gb_m()
            b = (s - 5) // 2
            if even and ok(b):
                tback(b, 1 if b > 0 else 2)
            if s in passes:
                mm(passes[s])
            if ok(b):
                if even:
                    residual(b, 1)
                else:
                    tback_open(b, "tb")
                    residual(b, 0)

            evac(s, 0, False)
            if not head:
                evac(s, 1, False)
            if s == 2:
                regroup_w(1, "s")
            if s in passes:
                relu(passes[s])

            if head:
                evac(s, 1, True)
            if even:
                if s >= 1:
                    quant(s - 1)
                if ok((s - 8) // 2):
                    norm1((s - 8) // 2)
                    norm2((s - 8) // 2)
                if s == 2:
                    regroup_w(0, "v")
                    quant_w(0)
                    quant_w(1)
                    const_bias_c()
                if s == 4:
                    regroup_w(3, "v")
                    quant_w(2)
                    quant_w(3)
            else:
                quant(s - 1)
                if s == 3:
                    regroup_w(2, "v")
                    const_gb_c()
                if ok((s - 7) // 2):
                    stats((s - 7) // 2)
                if s in sums:
                    hsum(sums[s])
                if ok((s - 7) // 2):
                    aggr((s - 7) // 2)
                    rsqrt((s - 7) // 2)

        quant(2 * L + 1)
        norm1(L - 3)
        tback(L - 2, 1)
        residual(L - 2, 1)
        norm2(L - 3)
        stats(L - 2)
        for s in range(NSTEP - LAG, NSTEP):
            mm(s)
            relu(s)
        aggr(L - 2)
        rsqrt(L - 2)
        for b in (L - 1, L):
            tback_open(b, "tf")
            residual(b, 0)
            tback(b, 2)
            residual(b, 1)
        norm1(L - 2)
        for b in (L - 1, L):
            stats(b)
            norm2(b - 1)
            aggr(b)
            rsqrt(b)
            norm1(b)
        norm2(L)
